import numpy as np
import ml_dtypes

BF16 = ml_dtypes.bfloat16


def bf(x):
    return np.asarray(x, np.float32).astype(BF16)


def f32(x):
    return np.asarray(x, np.float32)


def f64(x):
    return np.asarray(x).astype(np.float64)


def striped(idx):
    return np.tile(idx.reshape(-1, 16).T, (8, 1))


D, S, N, P = 128, 4096, 2048, 1024


def setup_inputs():
    return {
        "table": bf(np.random.standard_normal((D, S))),
        "w1": bf(np.random.standard_normal((D, D)) / np.sqrt(D)),
        "b1": f32(0.1 * np.random.standard_normal((D, 1))),
        "w2": bf(np.random.standard_normal((D, D)) * np.sqrt(2.0 / D)),
        "b2": f32(0.1 * np.random.standard_normal((D, 1))),
        "wb": f32(1.0 + 0.1 * np.random.standard_normal((D, 1))),
        "ob": f32(0.1 * np.random.standard_normal((D, 1))),
        "wc1": bf(np.random.standard_normal((D, D)) / np.sqrt(D)),
        "bc1": f32(0.1 * np.random.standard_normal((D, 1))),
        "offs": striped(np.random.permutation(np.tile(np.arange(S), 2))[:N]),
    }


def reference(table, w1, b1, w2, b2, wb, ob, wc1, bc1, offs):
    idx = offs[:16].T.reshape(-1)
    a = np.maximum(f64(w1).T @ f64(table)[:, idx] + f64(b1), 0.0)
    h = f64(w2).T @ a + f64(b2)
    t = f64(wb) * h
    z = t[:, :P] * t[:, P:] + f64(ob)
    return np.maximum(f64(wc1).T @ z + f64(bc1), 0.0)

@@ -1,0 +1,76 @@
+import concourse.mybir as mybir
+
+BF16, F32, U16 = mybir.dt.bfloat16, mybir.dt.float32, mybir.dt.uint16
+RELU = mybir.ActivationFunctionType.Relu
+ADD, MULT = mybir.AluOpType.add, mybir.AluOpType.mult
+
+D = 128
+GENES = 4096
+PAIRS = 1024
+N = 2 * PAIRS
+CHUNK = 512
+FLOPS = 2 * D * D * (N + N + PAIRS)
+
+
+def tile_bilinearmlpembedpheno_kernel(tc, table, w1, b1, w2, b2, wb, ob, wc1, bc1, offs, out):
+    nc = tc.nc
+    with (
+        tc.tile_pool(name="held", bufs=1) as held,
+        tc.tile_pool(name="work", bufs=2) as work,
+        tc.psum_pool(name="psum", bufs=8) as psum,
+    ):
+        offsets = held.tile([D, N // 16], U16, name="offsets")
+        nc.sync.dma_start(offsets[:], offs)
+        table_sb = held.tile([D, GENES], BF16, name="table_sb")
+        nc.sync.dma_start(table_sb[:], table)
+
+        w1_sb = held.tile([D, D], BF16, name="w1_sb")
+        w2_sb = held.tile([D, D], BF16, name="w2_sb")
+        wc1_sb = held.tile([D, D], BF16, name="wc1_sb")
+        b1_sb = held.tile([D, 1], F32, name="b1_sb")
+        b2_sb = held.tile([D, 1], F32, name="b2_sb")
+        wb_sb = held.tile([D, 1], F32, name="wb_sb")
+        ob_sb = held.tile([D, 1], F32, name="ob_sb")
+        bc1_sb = held.tile([D, 1], F32, name="bc1_sb")
+        for tile_sb, source in (
+            (w1_sb, w1),
+            (b1_sb, b1),
+            (w2_sb, w2),
+            (b2_sb, b2),
+            (wb_sb, wb),
+            (ob_sb, ob),
+            (wc1_sb, wc1),
+            (bc1_sb, bc1),
+        ):
+            nc.scalar.dma_start(tile_sb[:], source)
+
+        projected = {}
+        for c in range(PAIRS // CHUNK):
+            for side in range(2):
+                first = side * PAIRS + c * CHUNK
+                piece = offsets[:, first // 16 : (first + CHUNK) // 16]
+                proj = psum.tile([D, CHUNK], F32, name="proj", tag="bank")
+                nc.tensor.matmul(proj[:], w1_sb[:], table_sb[:].indirect(piece), start=True, stop=True)
+                projected[c, side] = proj
+
+        for c in range(PAIRS // CHUNK):
+            hidden = []
+            for side in range(2):
+                act = work.tile([D, CHUNK], BF16, name="act")
+                nc.scalar.activation(act[:], projected[c, side][:], RELU, bias=b1_sb[:])
+                hid = psum.tile([D, CHUNK], F32, name="hid", tag="bank")
+                nc.tensor.matmul(hid[:], w2_sb[:], act[:], start=True, stop=True)
+                hidden.append(hid)
+
+            t_first = work.tile([D, CHUNK], F32, name="t_first")
+            nc.vector.tensor_scalar(t_first[:], hidden[0][:], b2_sb[:], wb_sb[:], ADD, MULT)
+            prod = work.tile([D, CHUNK], F32, name="prod")
+            nc.vector.scalar_tensor_tensor(prod[:], hidden[1][:], b2_sb[:], t_first[:], ADD, MULT)
+            z = work.tile([D, CHUNK], BF16, name="z")
+            nc.vector.tensor_scalar(z[:], prod[:], wb_sb[:], ob_sb[:], MULT, ADD)
+
+            comb = psum.tile([D, CHUNK], F32, name="comb", tag="bank")
+            nc.tensor.matmul(comb[:], wc1_sb[:], z[:], start=True, stop=True)
+            res = work.tile([D, CHUNK], F32, name="res")
+            nc.scalar.activation(res[:], comb[:], RELU, bias=bc1_sb[:])
+            nc.sync.dma_start(out[:, c * CHUNK : (c + 1) * CHUNK], res[:])

@@ -2,13 +2,15 @@ import concourse.mybir as mybir
 
 BF16, F32, U16 = mybir.dt.bfloat16, mybir.dt.float32, mybir.dt.uint16
 RELU = mybir.ActivationFunctionType.Relu
-ADD, MULT = mybir.AluOpType.add, mybir.AluOpType.mult
+IDENTITY = mybir.ActivationFunctionType.Identity
+ADD, MULT, MAX = mybir.AluOpType.add, mybir.AluOpType.mult, mybir.AluOpType.max
 
 D = 128
 GENES = 4096
 PAIRS = 1024
 N = 2 * PAIRS
-CHUNK = 512
+CHUNK = 256
+CHUNKS = PAIRS // CHUNK
 FLOPS = 2 * D * D * (N + N + PAIRS)
 
 
@@ -16,7 +18,7 @@ def tile_bilinearmlpembedpheno_kernel(tc, table, w1, b1, w2, b2, wb, ob, wc1, bc
     nc = tc.nc
     with (
         tc.tile_pool(name="held", bufs=1) as held,
-        tc.tile_pool(name="work", bufs=2) as work,
+        tc.tile_pool(name="work", bufs=CHUNKS) as work,
         tc.psum_pool(name="psum", bufs=8) as psum,
     ):
         offsets = held.tile([D, N // 16], U16, name="offsets")
@@ -32,45 +34,55 @@ def tile_bilinearmlpembedpheno_kernel(tc, table, w1, b1, w2, b2, wb, ob, wc1, bc
         wb_sb = held.tile([D, 1], F32, name="wb_sb")
         ob_sb = held.tile([D, 1], F32, name="ob_sb")
         bc1_sb = held.tile([D, 1], F32, name="bc1_sb")
-        for tile_sb, source in (
-            (w1_sb, w1),
-            (b1_sb, b1),
-            (w2_sb, w2),
-            (b2_sb, b2),
-            (wb_sb, wb),
-            (ob_sb, ob),
-            (wc1_sb, wc1),
-            (bc1_sb, bc1),
-        ):
+        for tile_sb, source in ((w1_sb, w1), (b1_sb, b1), (w2_sb, w2), (b2_sb, b2), (wb_sb, wb)):
             nc.scalar.dma_start(tile_sb[:], source)
+        for tile_sb, source in ((ob_sb, ob), (wc1_sb, wc1), (bc1_sb, bc1)):
+            nc.sync.dma_start(tile_sb[:], source)
 
-        projected = {}
-        for c in range(PAIRS // CHUNK):
+        scratch = held.tile([D, 1], F32, name="scratch")
+        nc.vector.memset(scratch[:], 0.0)
+        nc.scalar.activation(scratch[:], scratch[:], RELU)
+
+        activated = []
+        for c in range(CHUNKS):
+            act = work.tile([D, 2 * CHUNK], BF16, name="act")
             for side in range(2):
                 first = side * PAIRS + c * CHUNK
                 piece = offsets[:, first // 16 : (first + CHUNK) // 16]
                 proj = psum.tile([D, CHUNK], F32, name="proj", tag="bank")
                 nc.tensor.matmul(proj[:], w1_sb[:], table_sb[:].indirect(piece), start=True, stop=True)
-                projected[c, side] = proj
+                half = act[:, side * CHUNK : (side + 1) * CHUNK]
+                if side == 0:
+                    nc.scalar.activation(half, proj[:], RELU, bias=b1_sb[:])
+                else:
+                    nc.vector.tensor_scalar(half, proj[:], b1_sb[:], 0.0, ADD, MAX)
+            activated.append(act)
 
-        for c in range(PAIRS // CHUNK):
-            hidden = []
-            for side in range(2):
-                act = work.tile([D, CHUNK], BF16, name="act")
-                nc.scalar.activation(act[:], projected[c, side][:], RELU, bias=b1_sb[:])
-                hid = psum.tile([D, CHUNK], F32, name="hid", tag="bank")
-                nc.tensor.matmul(hid[:], w2_sb[:], act[:], start=True, stop=True)
-                hidden.append(hid)
+        wb_b2 = held.tile([D, 1], F32, name="wb_b2")
+        nc.vector.tensor_tensor(wb_b2[:], wb_sb[:], b2_sb[:], MULT)
 
+
+        hidden = []
+        firsts = []
+        for c in range(CHUNKS):
+            hid = psum.tile([D, 2 * CHUNK], F32, name="hid", tag="bank")
+            nc.tensor.matmul(hid[:], w2_sb[:], activated[c][:], start=True, stop=True)
             t_first = work.tile([D, CHUNK], F32, name="t_first")
-            nc.vector.tensor_scalar(t_first[:], hidden[0][:], b2_sb[:], wb_sb[:], ADD, MULT)
+            nc.scalar.activation(t_first[:], hid[:, 0:CHUNK], IDENTITY, bias=wb_b2[:], scale=wb_sb[:])
+            hidden.append(hid)
+            firsts.append(t_first)
+
+        joined = []
+        for c in range(CHUNKS):
             prod = work.tile([D, CHUNK], F32, name="prod")
-            nc.vector.scalar_tensor_tensor(prod[:], hidden[1][:], b2_sb[:], t_first[:], ADD, MULT)
+            nc.vector.scalar_tensor_tensor(prod[:], hidden[c][:, CHUNK : 2 * CHUNK], b2_sb[:], firsts[c][:], ADD, MULT)
             z = work.tile([D, CHUNK], BF16, name="z")
             nc.vector.tensor_scalar(z[:], prod[:], wb_sb[:], ob_sb[:], MULT, ADD)
+            joined.append(z)
 
+        for c in range(CHUNKS):
             comb = psum.tile([D, CHUNK], F32, name="comb", tag="bank")
-            nc.tensor.matmul(comb[:], wc1_sb[:], z[:], start=True, stop=True)
+            nc.tensor.matmul(comb[:], wc1_sb[:], joined[c][:], start=True, stop=True)
             res = work.tile([D, CHUNK], F32, name="res")
             nc.scalar.activation(res[:], comb[:], RELU, bias=bc1_sb[:])
             nc.sync.dma_start(out[:, c * CHUNK : (c + 1) * CHUNK], res[:])

@@ -11,6 +11,7 @@ PAIRS = 1024
 N = 2 * PAIRS
 CHUNK = 256
 CHUNKS = PAIRS // CHUNK
+WARM_UP = 8
 FLOPS = 2 * D * D * (N + N + PAIRS)
 
 
@@ -42,6 +43,12 @@ def tile_bilinearmlpembedpheno_kernel(tc, table, w1, b1, w2, b2, wb, ob, wc1, bc
         scratch = held.tile([D, 1], F32, name="scratch")
         nc.vector.memset(scratch[:], 0.0)
         nc.scalar.activation(scratch[:], scratch[:], RELU)
+
+        zeros = held.tile([D, 512], BF16, name="zeros")
+        nc.vector.memset(zeros[:], 0.0)
+        unread = psum.tile([D, 512], F32, name="unread", tag="bank")
+        for i in range(WARM_UP):
+            nc.tensor.matmul(unread[:], zeros[:, 0:D], zeros[:], start=True, stop=True)
 
         activated = []
         for c in range(CHUNKS):

@@ -11,7 +11,6 @@ PAIRS = 1024
 N = 2 * PAIRS
 CHUNK = 256
 CHUNKS = PAIRS // CHUNK
-WARM_UP = 8
 FLOPS = 2 * D * D * (N + N + PAIRS)
 
 
@@ -44,12 +43,6 @@ def tile_bilinearmlpembedpheno_kernel(tc, table, w1, b1, w2, b2, wb, ob, wc1, bc
         nc.vector.memset(scratch[:], 0.0)
         nc.scalar.activation(scratch[:], scratch[:], RELU)
 
-        zeros = held.tile([D, 512], BF16, name="zeros")
-        nc.vector.memset(zeros[:], 0.0)
-        unread = psum.tile([D, 512], F32, name="unread", tag="bank")
-        for i in range(WARM_UP):
-            nc.tensor.matmul(unread[:], zeros[:, 0:D], zeros[:], start=True, stop=True)
-
         activated = []
         for c in range(CHUNKS):
             act = work.tile([D, 2 * CHUNK], BF16, name="act")
@@ -79,13 +72,19 @@ def tile_bilinearmlpembedpheno_kernel(tc, table, w1, b1, w2, b2, wb, ob, wc1, bc
             hidden.append(hid)
             firsts.append(t_first)
 
+        products = []
         joined = []
-        for c in range(CHUNKS):
-            prod = work.tile([D, CHUNK], F32, name="prod")
-            nc.vector.scalar_tensor_tensor(prod[:], hidden[c][:, CHUNK : 2 * CHUNK], b2_sb[:], firsts[c][:], ADD, MULT)
-            z = work.tile([D, CHUNK], BF16, name="z")
-            nc.vector.tensor_scalar(z[:], prod[:], wb_sb[:], ob_sb[:], MULT, ADD)
-            joined.append(z)
+        for c in range(CHUNKS + 1):
+            if c < CHUNKS:
+                prod = work.tile([D, CHUNK], F32, name="prod")
+                nc.vector.scalar_tensor_tensor(
+                    prod[:], hidden[c][:, CHUNK : 2 * CHUNK], b2_sb[:], firsts[c][:], ADD, MULT
+                )
+                products.append(prod)
+            if c > 0:
+                z = work.tile([D, CHUNK], BF16, name="z")
+                nc.vector.tensor_scalar(z[:], products[c - 1][:], wb_sb[:], ob_sb[:], MULT, ADD)
+                joined.append(z)
 
         for c in range(CHUNKS):
             comb = psum.tile([D, CHUNK], F32, name="comb", tag="bank")

@@ -34,9 +34,9 @@ def tile_bilinearmlpembedpheno_kernel(tc, table, w1, b1, w2, b2, wb, ob, wc1, bc
         wb_sb = held.tile([D, 1], F32, name="wb_sb")
         ob_sb = held.tile([D, 1], F32, name="ob_sb")
         bc1_sb = held.tile([D, 1], F32, name="bc1_sb")
-        for tile_sb, source in ((w1_sb, w1), (b1_sb, b1), (w2_sb, w2), (b2_sb, b2), (wb_sb, wb)):
+        for tile_sb, source in ((w1_sb, w1), (b1_sb, b1), (w2_sb, w2)):
             nc.scalar.dma_start(tile_sb[:], source)
-        for tile_sb, source in ((ob_sb, ob), (wc1_sb, wc1), (bc1_sb, bc1)):
+        for tile_sb, source in ((b2_sb, b2), (wb_sb, wb), (ob_sb, ob), (wc1_sb, wc1), (bc1_sb, bc1)):
             nc.sync.dma_start(tile_sb[:], source)
 
         scratch = held.tile([D, 1], F32, name="scratch")
@@ -72,23 +72,17 @@ def tile_bilinearmlpembedpheno_kernel(tc, table, w1, b1, w2, b2, wb, ob, wc1, bc
             hidden.append(hid)
             firsts.append(t_first)
 
-        products = []
         joined = []
-        for c in range(CHUNKS + 1):
-            if c < CHUNKS:
-                prod = work.tile([D, CHUNK], F32, name="prod")
-                nc.vector.scalar_tensor_tensor(
-                    prod[:], hidden[c][:, CHUNK : 2 * CHUNK], b2_sb[:], firsts[c][:], ADD, MULT
-                )
-                products.append(prod)
-            if c > 0:
-                z = work.tile([D, CHUNK], BF16, name="z")
-                nc.vector.tensor_scalar(z[:], products[c - 1][:], wb_sb[:], ob_sb[:], MULT, ADD)
-                joined.append(z)
+        for c in range(CHUNKS):
+            prod = work.tile([D, CHUNK], F32, name="prod")
+            nc.vector.scalar_tensor_tensor(prod[:], hidden[c][:, CHUNK : 2 * CHUNK], b2_sb[:], firsts[c][:], ADD, MULT)
+            z = work.tile([D, CHUNK], BF16, name="z")
+            nc.scalar.activation(z[:], prod[:], IDENTITY, bias=ob_sb[:], scale=wb_sb[:])
+            joined.append(z)
 
         for c in range(CHUNKS):
             comb = psum.tile([D, CHUNK], F32, name="comb", tag="bank")
             nc.tensor.matmul(comb[:], wc1_sb[:], joined[c][:], start=True, stop=True)
             res = work.tile([D, CHUNK], F32, name="res")
-            nc.scalar.activation(res[:], comb[:], RELU, bias=bc1_sb[:])
+            nc.vector.tensor_scalar(res[:], comb[:], bc1_sb[:], 0.0, ADD, MAX)
             nc.sync.dma_start(out[:, c * CHUNK : (c + 1) * CHUNK], res[:])

@@ -77,12 +77,18 @@ def tile_bilinearmlpembedpheno_kernel(tc, table, w1, b1, w2, b2, wb, ob, wc1, bc
             prod = work.tile([D, CHUNK], F32, name="prod")
             nc.vector.scalar_tensor_tensor(prod[:], hidden[c][:, CHUNK : 2 * CHUNK], b2_sb[:], firsts[c][:], ADD, MULT)
             z = work.tile([D, CHUNK], BF16, name="z")
-            nc.scalar.activation(z[:], prod[:], IDENTITY, bias=ob_sb[:], scale=wb_sb[:])
+            if c % 2 == 0:
+                nc.scalar.activation(z[:], prod[:], IDENTITY, bias=ob_sb[:], scale=wb_sb[:])
+            else:
+                nc.vector.tensor_scalar(z[:], prod[:], wb_sb[:], ob_sb[:], MULT, ADD)
             joined.append(z)
 
         for c in range(CHUNKS):
             comb = psum.tile([D, CHUNK], F32, name="comb", tag="bank")
             nc.tensor.matmul(comb[:], wc1_sb[:], joined[c][:], start=True, stop=True)
             res = work.tile([D, CHUNK], F32, name="res")
-            nc.vector.tensor_scalar(res[:], comb[:], bc1_sb[:], 0.0, ADD, MAX)
+            if c % 2 == 0:
+                nc.scalar.activation(res[:], comb[:], RELU, bias=bc1_sb[:])
+            else:
+                nc.vector.tensor_scalar(res[:], comb[:], bc1_sb[:], 0.0, ADD, MAX)
             nc.sync.dma_start(out[:, c * CHUNK : (c + 1) * CHUNK], res[:])

@@ -9,8 +9,10 @@ D = 128
 GENES = 4096
 PAIRS = 1024
 N = 2 * PAIRS
-CHUNK = 256
-CHUNKS = PAIRS // CHUNK
+WIDTHS = (256, 256, 256, 256)
+STARTS = tuple(sum(WIDTHS[:c]) for c in range(len(WIDTHS)))
+CHUNKS = len(WIDTHS)
+assert sum(WIDTHS) == PAIRS
 FLOPS = 2 * D * D * (N + N + PAIRS)
 
 
@@ -44,19 +46,20 @@ def tile_bilinearmlpembedpheno_kernel(tc, table, w1, b1, w2, b2, wb, ob, wc1, bc
         nc.scalar.activation(scratch[:], scratch[:], RELU)
 
         activated = []
-        for c in range(CHUNKS):
-            act = work.tile([D, 2 * CHUNK], BF16, name="act")
+        for start, width in zip(STARTS, WIDTHS):
+            sides = []
             for side in range(2):
-                first = side * PAIRS + c * CHUNK
-                piece = offsets[:, first // 16 : (first + CHUNK) // 16]
-                proj = psum.tile([D, CHUNK], F32, name="proj", tag="bank")
+                first = side * PAIRS + start
+                piece = offsets[:, first // 16 : (first + width) // 16]
+                proj = psum.tile([D, width], F32, name="proj", tag="bank")
                 nc.tensor.matmul(proj[:], w1_sb[:], table_sb[:].indirect(piece), start=True, stop=True)
-                half = act[:, side * CHUNK : (side + 1) * CHUNK]
+                act = work.tile([D, width], BF16, name="act", tag="act%d" % side)
                 if side == 0:
-                    nc.scalar.activation(half, proj[:], RELU, bias=b1_sb[:])
+                    nc.scalar.activation(act[:], proj[:], RELU, bias=b1_sb[:])
                 else:
-                    nc.vector.tensor_scalar(half, proj[:], b1_sb[:], 0.0, ADD, MAX)
-            activated.append(act)
+                    nc.vector.tensor_scalar(act[:], proj[:], b1_sb[:], 0.0, ADD, MAX)
+                sides.append(act)
+            activated.append(sides)
 
         wb_b2 = held.tile([D, 1], F32, name="wb_b2")
         nc.vector.tensor_tensor(wb_b2[:], wb_sb[:], b2_sb[:], MULT)
@@ -64,31 +67,33 @@ def tile_bilinearmlpembedpheno_kernel(tc, table, w1, b1, w2, b2, wb, ob, wc1, bc
 
         hidden = []
         firsts = []
-        for c in range(CHUNKS):
-            hid = psum.tile([D, 2 * CHUNK], F32, name="hid", tag="bank")
-            nc.tensor.matmul(hid[:], w2_sb[:], activated[c][:], start=True, stop=True)
-            t_first = work.tile([D, CHUNK], F32, name="t_first")
-            nc.scalar.activation(t_first[:], hid[:, 0:CHUNK], IDENTITY, bias=wb_b2[:], scale=wb_sb[:])
-            hidden.append(hid)
+        for c, width in enumerate(WIDTHS):
+            hid_first = psum.tile([D, width], F32, name="hid_first", tag="bank")
+            nc.tensor.matmul(hid_first[:], w2_sb[:], activated[c][0][:], start=True, stop=True)
+            hid_second = psum.tile([D, width], F32, name="hid_second", tag="bank")
+            nc.tensor.matmul(hid_second[:], w2_sb[:], activated[c][1][:], start=True, stop=True)
+            t_first = work.tile([D, width], F32, name="t_first")
+            nc.scalar.activation(t_first[:], hid_first[:], IDENTITY, bias=wb_b2[:], scale=wb_sb[:])
+            hidden.append(hid_second)
             firsts.append(t_first)
 
         joined = []
-        for c in range(CHUNKS):
-            prod = work.tile([D, CHUNK], F32, name="prod")
-            nc.vector.scalar_tensor_tensor(prod[:], hidden[c][:, CHUNK : 2 * CHUNK], b2_sb[:], firsts[c][:], ADD, MULT)
-            z = work.tile([D, CHUNK], BF16, name="z")
-            if c % 2 == 0:
+        for c, width in enumerate(WIDTHS):
+            prod = work.tile([D, width], F32, name="prod")
+            nc.vector.scalar_tensor_tensor(prod[:], hidden[c][:], b2_sb[:], firsts[c][:], ADD, MULT)
+            z = work.tile([D, width], BF16, name="z")
+            if c < CHUNKS - 1:
                 nc.scalar.activation(z[:], prod[:], IDENTITY, bias=ob_sb[:], scale=wb_sb[:])
             else:
                 nc.vector.tensor_scalar(z[:], prod[:], wb_sb[:], ob_sb[:], MULT, ADD)
             joined.append(z)
 
-        for c in range(CHUNKS):
-            comb = psum.tile([D, CHUNK], F32, name="comb", tag="bank")
+        for c, (start, width) in enumerate(zip(STARTS, WIDTHS)):
+            comb = psum.tile([D, width], F32, name="comb", tag="bank")
             nc.tensor.matmul(comb[:], wc1_sb[:], joined[c][:], start=True, stop=True)
-            res = work.tile([D, CHUNK], F32, name="res")
-            if c % 2 == 0:
+            res = work.tile([D, width], F32, name="res")
+            if 0 < c < CHUNKS - 1:
                 nc.scalar.activation(res[:], comb[:], RELU, bias=bc1_sb[:])
             else:
                 nc.vector.tensor_scalar(res[:], comb[:], bc1_sb[:], 0.0, ADD, MAX)
-            nc.sync.dma_start(out[:, c * CHUNK : (c + 1) * CHUNK], res[:])
+            nc.sync.dma_start(out[:, start : start + width], res[:])

@@ -36,9 +36,9 @@ def tile_bilinearmlpembedpheno_kernel(tc, table, w1, b1, w2, b2, wb, ob, wc1, bc
         wb_sb = held.tile([D, 1], F32, name="wb_sb")
         ob_sb = held.tile([D, 1], F32, name="ob_sb")
         bc1_sb = held.tile([D, 1], F32, name="bc1_sb")
-        for tile_sb, source in ((w1_sb, w1), (b1_sb, b1), (w2_sb, w2)):
+        for tile_sb, source in ((w1_sb, w1), (b1_sb, b1)):
             nc.scalar.dma_start(tile_sb[:], source)
-        for tile_sb, source in ((b2_sb, b2), (wb_sb, wb), (ob_sb, ob), (wc1_sb, wc1), (bc1_sb, bc1)):
+        for tile_sb, source in ((w2_sb, w2), (b2_sb, b2), (wb_sb, wb), (wc1_sb, wc1), (ob_sb, ob), (bc1_sb, bc1)):
             nc.sync.dma_start(tile_sb[:], source)
 
         scratch = held.tile([D, 1], F32, name="scratch")
@@ -61,8 +61,8 @@ def tile_bilinearmlpembedpheno_kernel(tc, table, w1, b1, w2, b2, wb, ob, wc1, bc
                 sides.append(act)
             activated.append(sides)
 
-        wb_b2 = held.tile([D, 1], F32, name="wb_b2")
-        nc.vector.tensor_tensor(wb_b2[:], wb_sb[:], b2_sb[:], MULT)
+        wb_wb = held.tile([D, 1], F32, name="wb_wb")
+        nc.vector.tensor_tensor(wb_wb[:], wb_sb[:], wb_sb[:], MULT)
 
 
         hidden = []
@@ -72,10 +72,10 @@ def tile_bilinearmlpembedpheno_kernel(tc, table, w1, b1, w2, b2, wb, ob, wc1, bc
             nc.tensor.matmul(hid_first[:], w2_sb[:], activated[c][0][:], start=True, stop=True)
             hid_second = psum.tile([D, width], F32, name="hid_second", tag="bank")
             nc.tensor.matmul(hid_second[:], w2_sb[:], activated[c][1][:], start=True, stop=True)
-            t_first = work.tile([D, width], F32, name="t_first")
-            nc.scalar.activation(t_first[:], hid_first[:], IDENTITY, bias=wb_b2[:], scale=wb_sb[:])
+            h_first = work.tile([D, width], F32, name="h_first")
+            nc.scalar.activation(h_first[:], hid_first[:], IDENTITY, bias=b2_sb[:])
             hidden.append(hid_second)
-            firsts.append(t_first)
+            firsts.append(h_first)
 
         joined = []
         for c, width in enumerate(WIDTHS):
@@ -83,9 +83,9 @@ def tile_bilinearmlpembedpheno_kernel(tc, table, w1, b1, w2, b2, wb, ob, wc1, bc
             nc.vector.scalar_tensor_tensor(prod[:], hidden[c][:], b2_sb[:], firsts[c][:], ADD, MULT)
             z = work.tile([D, width], BF16, name="z")
             if c < CHUNKS - 1:
-                nc.scalar.activation(z[:], prod[:], IDENTITY, bias=ob_sb[:], scale=wb_sb[:])
+                nc.scalar.activation(z[:], prod[:], IDENTITY, bias=ob_sb[:], scale=wb_wb[:])
             else:
-                nc.vector.tensor_scalar(z[:], prod[:], wb_sb[:], ob_sb[:], MULT, ADD)
+                nc.vector.tensor_scalar(z[:], prod[:], wb_wb[:], ob_sb[:], MULT, ADD)
             joined.append(z)
 
         for c, (start, width) in enumerate(zip(STARTS, WIDTHS)):

@@ -9,10 +9,11 @@ D = 128
 GENES = 4096
 PAIRS = 1024
 N = 2 * PAIRS
-WIDTHS = (256, 256, 256, 256)
-STARTS = tuple(sum(WIDTHS[:c]) for c in range(len(WIDTHS)))
-CHUNKS = len(WIDTHS)
-assert sum(WIDTHS) == PAIRS
+GROUPS = ((0, 512), (512, 256), (768, 256))
+CHUNK = 256
+CHUNKS = PAIRS // CHUNK
+WIDTHS = (CHUNK,) * CHUNKS
+STARTS = tuple(range(0, PAIRS, CHUNK))
 FLOPS = 2 * D * D * (N + N + PAIRS)
 
 
@@ -46,7 +47,7 @@ def tile_bilinearmlpembedpheno_kernel(tc, table, w1, b1, w2, b2, wb, ob, wc1, bc
         nc.scalar.activation(scratch[:], scratch[:], RELU)
 
         activated = []
-        for start, width in zip(STARTS, WIDTHS):
+        for start, width in GROUPS:
             sides = []
             for side in range(2):
                 first = side * PAIRS + start
@@ -59,7 +60,8 @@ def tile_bilinearmlpembedpheno_kernel(tc, table, w1, b1, w2, b2, wb, ob, wc1, bc
                 else:
                     nc.vector.tensor_scalar(act[:], proj[:], b1_sb[:], 0.0, ADD, MAX)
                 sides.append(act)
-            activated.append(sides)
+            for column in range(0, width, CHUNK):
+                activated.append([act[:, column : column + CHUNK] for act in sides])
 
         wb_wb = held.tile([D, 1], F32, name="wb_wb")
         nc.vector.tensor_tensor(wb_wb[:], wb_sb[:], wb_sb[:], MULT)
@@ -69,9 +71,9 @@ def tile_bilinearmlpembedpheno_kernel(tc, table, w1, b1, w2, b2, wb, ob, wc1, bc
         firsts = []
         for c, width in enumerate(WIDTHS):
             hid_first = psum.tile([D, width], F32, name="hid_first", tag="bank")
-            nc.tensor.matmul(hid_first[:], w2_sb[:], activated[c][0][:], start=True, stop=True)
+            nc.tensor.matmul(hid_first[:], w2_sb[:], activated[c][0], start=True, stop=True)
             hid_second = psum.tile([D, width], F32, name="hid_second", tag="bank")
-            nc.tensor.matmul(hid_second[:], w2_sb[:], activated[c][1][:], start=True, stop=True)
+            nc.tensor.matmul(hid_second[:], w2_sb[:], activated[c][1], start=True, stop=True)
             h_first = work.tile([D, width], F32, name="h_first")
             nc.scalar.activation(h_first[:], hid_first[:], IDENTITY, bias=b2_sb[:])
             hidden.append(hid_second)

@@ -69,15 +69,17 @@ def tile_bilinearmlpembedpheno_kernel(tc, table, w1, b1, w2, b2, wb, ob, wc1, bc
 
         hidden = []
         firsts = []
-        for c, width in enumerate(WIDTHS):
-            hid_first = psum.tile([D, width], F32, name="hid_first", tag="bank")
-            nc.tensor.matmul(hid_first[:], w2_sb[:], activated[c][0], start=True, stop=True)
-            hid_second = psum.tile([D, width], F32, name="hid_second", tag="bank")
-            nc.tensor.matmul(hid_second[:], w2_sb[:], activated[c][1], start=True, stop=True)
-            h_first = work.tile([D, width], F32, name="h_first")
-            nc.scalar.activation(h_first[:], hid_first[:], IDENTITY, bias=b2_sb[:])
-            hidden.append(hid_second)
-            firsts.append(h_first)
+        for step in range(CHUNKS + 1):
+            if step < CHUNKS:
+                hid_first = psum.tile([D, WIDTHS[step]], F32, name="hid_first", tag="bank")
+                nc.tensor.matmul(hid_first[:], w2_sb[:], activated[step][0], start=True, stop=True)
+                h_first = work.tile([D, WIDTHS[step]], F32, name="h_first")
+                nc.scalar.activation(h_first[:], hid_first[:], IDENTITY, bias=b2_sb[:])
+                firsts.append(h_first)
+            if step > 0:
+                hid_second = psum.tile([D, WIDTHS[step - 1]], F32, name="hid_second", tag="bank")
+                nc.tensor.matmul(hid_second[:], w2_sb[:], activated[step - 1][1], start=True, stop=True)
+                hidden.append(hid_second)
 
         joined = []
         for c, width in enumerate(WIDTHS):

@@ -71,10 +71,14 @@ def tile_bilinearmlpembedpheno_kernel(tc, table, w1, b1, w2, b2, wb, ob, wc1, bc
         firsts = []
         for step in range(CHUNKS + 1):
             if step < CHUNKS:
-                hid_first = psum.tile([D, WIDTHS[step]], F32, name="hid_first", tag="bank")
-                nc.tensor.matmul(hid_first[:], w2_sb[:], activated[step][0], start=True, stop=True)
                 h_first = work.tile([D, WIDTHS[step]], F32, name="h_first")
-                nc.scalar.activation(h_first[:], hid_first[:], IDENTITY, bias=b2_sb[:])
+                parts = 2 if step == 0 else 1
+                part_width = WIDTHS[step] // parts
+                for low in range(0, WIDTHS[step], part_width):
+                    columns = slice(low, low + part_width)
+                    hid_first = psum.tile([D, part_width], F32, name="hid_first", tag="bank")
+                    nc.tensor.matmul(hid_first[:], w2_sb[:], activated[step][0][:, columns], start=True, stop=True)
+                    nc.scalar.activation(h_first[:, columns], hid_first[:], IDENTITY, bias=b2_sb[:])
                 firsts.append(h_first)
             if step > 0:
                 hid_second = psum.tile([D, WIDTHS[step - 1]], F32, name="hid_second", tag="bank")

@@ -9,7 +9,7 @@ D = 128
 GENES = 4096
 PAIRS = 1024
 N = 2 * PAIRS
-GROUPS = ((0, 512), (512, 256), (768, 256))
+GATHERS = ((0, 0, 512), (1, 0, 512), (0, 512, 512), (1, 512, 256), (1, 768, 256))
 CHUNK = 256
 CHUNKS = PAIRS // CHUNK
 WIDTHS = (CHUNK,) * CHUNKS
@@ -46,22 +46,18 @@ def tile_bilinearmlpembedpheno_kernel(tc, table, w1, b1, w2, b2, wb, ob, wc1, bc
         nc.vector.memset(scratch[:], 0.0)
         nc.scalar.activation(scratch[:], scratch[:], RELU)
 
-        activated = []
-        for start, width in GROUPS:
-            sides = []
-            for side in range(2):
-                first = side * PAIRS + start
-                piece = offsets[:, first // 16 : (first + width) // 16]
-                proj = psum.tile([D, width], F32, name="proj", tag="bank")
-                nc.tensor.matmul(proj[:], w1_sb[:], table_sb[:].indirect(piece), start=True, stop=True)
-                act = work.tile([D, width], BF16, name="act", tag="act%d" % side)
-                if side == 0:
-                    nc.scalar.activation(act[:], proj[:], RELU, bias=b1_sb[:])
-                else:
-                    nc.vector.tensor_scalar(act[:], proj[:], b1_sb[:], 0.0, ADD, MAX)
-                sides.append(act)
-            for column in range(0, width, CHUNK):
-                activated.append([act[:, column : column + CHUNK] for act in sides])
+        activated = ([], [])
+        for side, start, width in GATHERS:
+            first = side * PAIRS + start
+            piece = offsets[:, first // 16 : (first + width) // 16]
+            proj = psum.tile([D, width], F32, name="proj", tag="bank")
+            nc.tensor.matmul(proj[:], w1_sb[:], table_sb[:].indirect(piece), start=True, stop=True)
+            act = work.tile([D, width], BF16, name="act", tag="act%d" % side)
+            if side == 0:
+                nc.scalar.activation(act[:], proj[:], RELU, bias=b1_sb[:])
+            else:
+                nc.vector.tensor_scalar(act[:], proj[:], b1_sb[:], 0.0, ADD, MAX)
+            activated[side].extend(act[:, column : column + CHUNK] for column in range(0, width, CHUNK))
 
         wb_wb = held.tile([D, 1], F32, name="wb_wb")
         nc.vector.tensor_tensor(wb_wb[:], wb_sb[:], wb_sb[:], MULT)
@@ -77,12 +73,12 @@ def tile_bilinearmlpembedpheno_kernel(tc, table, w1, b1, w2, b2, wb, ob, wc1, bc
                 for low in range(0, WIDTHS[step], part_width):
                     columns = slice(low, low + part_width)
                     hid_first = psum.tile([D, part_width], F32, name="hid_first", tag="bank")
-                    nc.tensor.matmul(hid_first[:], w2_sb[:], activated[step][0][:, columns], start=True, stop=True)
+                    nc.tensor.matmul(hid_first[:], w2_sb[:], activated[0][step][:, columns], start=True, stop=True)
                     nc.scalar.activation(h_first[:, columns], hid_first[:], IDENTITY, bias=b2_sb[:])
                 firsts.append(h_first)
             if step > 0:
                 hid_second = psum.tile([D, WIDTHS[step - 1]], F32, name="hid_second", tag="bank")
-                nc.tensor.matmul(hid_second[:], w2_sb[:], activated[step - 1][1], start=True, stop=True)
+                nc.tensor.matmul(hid_second[:], w2_sb[:], activated[1][step - 1], start=True, stop=True)
                 hidden.append(hid_second)
 
         joined = []

import concourse.mybir as mybir

BF16, F32, U16 = mybir.dt.bfloat16, mybir.dt.float32, mybir.dt.uint16
RELU = mybir.ActivationFunctionType.Relu
IDENTITY = mybir.ActivationFunctionType.Identity
ADD, MULT, MAX = mybir.AluOpType.add, mybir.AluOpType.mult, mybir.AluOpType.max

D = 128
GENES = 4096
PAIRS = 1024
N = 2 * PAIRS
GATHERS = ((0, 0, 512), (1, 0, 512), (0, 512, 512), (1, 512, 256), (1, 768, 256))
CHUNK = 256
CHUNKS = PAIRS // CHUNK
WIDTHS = (CHUNK,) * CHUNKS
STARTS = tuple(range(0, PAIRS, CHUNK))
FLOPS = 2 * D * D * (N + N + PAIRS)


def tile_bilinearmlpembedpheno_kernel(tc, table, w1, b1, w2, b2, wb, ob, wc1, bc1, offs, out):
    nc = tc.nc
    with (
        tc.tile_pool(name="held", bufs=1) as held,
        tc.tile_pool(name="work", bufs=CHUNKS) as work,
        tc.psum_pool(name="psum", bufs=8) as psum,
    ):
        offsets = held.tile([D, N // 16], U16, name="offsets")
        nc.sync.dma_start(offsets[:], offs)
        table_sb = held.tile([D, GENES], BF16, name="table_sb")
        nc.sync.dma_start(table_sb[:], table)

        w1_sb = held.tile([D, D], BF16, name="w1_sb")
        w2_sb = held.tile([D, D], BF16, name="w2_sb")
        wc1_sb = held.tile([D, D], BF16, name="wc1_sb")
        b1_sb = held.tile([D, 1], F32, name="b1_sb")
        b2_sb = held.tile([D, 1], F32, name="b2_sb")
        wb_sb = held.tile([D, 1], F32, name="wb_sb")
        ob_sb = held.tile([D, 1], F32, name="ob_sb")
        bc1_sb = held.tile([D, 1], F32, name="bc1_sb")
        for tile_sb, source in ((w1_sb, w1), (b1_sb, b1)):
            nc.scalar.dma_start(tile_sb[:], source)
        for tile_sb, source in ((w2_sb, w2), (b2_sb, b2), (wb_sb, wb), (wc1_sb, wc1), (ob_sb, ob), (bc1_sb, bc1)):
            nc.sync.dma_start(tile_sb[:], source)

        scratch = held.tile([D, 1], F32, name="scratch")
        nc.vector.memset(scratch[:], 0.0)
        nc.scalar.activation(scratch[:], scratch[:], RELU)

        activated = ([], [])
        for side, start, width in GATHERS:
            first = side * PAIRS + start
            piece = offsets[:, first // 16 : (first + width) // 16]
            proj = psum.tile([D, width], F32, name="proj", tag="bank")
            nc.tensor.matmul(proj[:], w1_sb[:], table_sb[:].indirect(piece), start=True, stop=True)
            act = work.tile([D, width], BF16, name="act", tag="act%d" % side)
            if side == 0:
                nc.scalar.activation(act[:], proj[:], RELU, bias=b1_sb[:])
            else:
                nc.vector.tensor_scalar(act[:], proj[:], b1_sb[:], 0.0, ADD, MAX)
            activated[side].extend(act[:, column : column + CHUNK] for column in range(0, width, CHUNK))

        wb_wb = held.tile([D, 1], F32, name="wb_wb")
        nc.vector.tensor_tensor(wb_wb[:], wb_sb[:], wb_sb[:], MULT)


        hidden = []
        firsts = []
        for step in range(CHUNKS + 1):
            if step < CHUNKS:
                h_first = work.tile([D, WIDTHS[step]], F32, name="h_first")
                parts = 2 if step == 0 else 1
                part_width = WIDTHS[step] // parts
                for low in range(0, WIDTHS[step], part_width):
                    columns = slice(low, low + part_width)
                    hid_first = psum.tile([D, part_width], F32, name="hid_first", tag="bank")
                    nc.tensor.matmul(hid_first[:], w2_sb[:], activated[0][step][:, columns], start=True, stop=True)
                    nc.scalar.activation(h_first[:, columns], hid_first[:], IDENTITY, bias=b2_sb[:])
                firsts.append(h_first)
            if step > 0:
                hid_second = psum.tile([D, WIDTHS[step - 1]], F32, name="hid_second", tag="bank")
                nc.tensor.matmul(hid_second[:], w2_sb[:], activated[1][step - 1], start=True, stop=True)
                hidden.append(hid_second)

        joined = []
        for c, width in enumerate(WIDTHS):
            prod = work.tile([D, width], F32, name="prod")
            nc.vector.scalar_tensor_tensor(prod[:], hidden[c][:], b2_sb[:], firsts[c][:], ADD, MULT)
            z = work.tile([D, width], BF16, name="z")
            if c < CHUNKS - 1:
                nc.scalar.activation(z[:], prod[:], IDENTITY, bias=ob_sb[:], scale=wb_wb[:])
            else:
                nc.vector.tensor_scalar(z[:], prod[:], wb_wb[:], ob_sb[:], MULT, ADD)
            joined.append(z)

        for c, (start, width) in enumerate(zip(STARTS, WIDTHS)):
            comb = psum.tile([D, width], F32, name="comb", tag="bank")
            nc.tensor.matmul(comb[:], wc1_sb[:], joined[c][:], start=True, stop=True)
            res = work.tile([D, width], F32, name="res")
            if 0 < c < CHUNKS - 1:
                nc.scalar.activation(res[:], comb[:], RELU, bias=bc1_sb[:])
            else:
                nc.vector.tensor_scalar(res[:], comb[:], bc1_sb[:], 0.0, ADD, MAX)
            nc.sync.dma_start(out[:, start : start + width], res[:])
